import numpy as np
import ml_dtypes


def mxq(x, axis, fmt="e4m3"):
    dtype, down = {"e4m3": (ml_dtypes.float8_e4m3fn, 7), "e5m2": (ml_dtypes.float8_e5m2, 14)}[fmt]
    v = np.moveaxis(np.asarray(x, np.float32).astype(ml_dtypes.bfloat16).astype(np.float64), axis, -1)
    blocks = v.reshape(v.shape[:-1] + (-1, 32))
    amax = np.abs(blocks).max(-1, keepdims=True)
    byte = np.maximum(np.where(amax > 0, np.frexp(amax)[1] - 1 + 127, 0) - down, 1)
    scale = np.exp2(byte - 127.0)
    codes = (blocks / scale).astype(np.float32).astype(dtype).astype(np.float64)
    return np.moveaxis((codes * scale).reshape(v.shape), -1, axis)


WIDE = False


def mx_kscale(k):
    if not WIDE:
        return np.ones(k)
    levels = np.array([10, -10, 5, -5, 0])
    if k % 512:
        return np.exp2(np.random.permutation(np.resize(levels, k // 32))).repeat(32)
    a = np.empty((k // 512, 16))
    for p in range(k // 512):
        a[p, :8] = np.random.permutation(np.resize(levels, 8))
        for g in range(8):
            far = levels[np.abs(levels - a[p, g]) >= 10]
            a[p, g + 8] = far[np.random.randint(len(far))]
    return np.exp2(a.ravel()).repeat(32)


BF16 = ml_dtypes.bfloat16


def bf(x):
    return np.asarray(x, np.float32).astype(BF16)


def f64(x):
    return np.asarray(x).astype(np.float64)


E2M1 = np.array([0.0, 0.5, 1.0, 1.5, 2.0, 3.0, 4.0, 6.0, -0.0, -0.5, -1.0, -1.5, -2.0, -3.0, -4.0, -6.0])


def pack_weight(w, fmt):
    k, n = w.shape
    w = f64(bf(w)).reshape(k // 32, 32, n)
    amax = np.abs(w).max(1)
    if fmt == "e4m3":
        byte = np.frexp(amax)[1] - 1 + 127 - 7
    else:
        mant, ex = np.frexp(amax / 6.0)
        byte = np.where(mant > 0.5, ex, ex - 1) + 127
    byte = np.clip(np.where(amax > 0, byte, 1), 1, 254)
    scaled = (w * np.exp2(127.0 - byte)[:, None, :]).reshape(k, n).astype(np.float32)
    by_word = np.ascontiguousarray(scaled.reshape(k // 512, 128, 4, n).transpose(0, 1, 3, 2))
    if fmt == "e4m3":
        words = by_word.astype(ml_dtypes.float8_e4m3fn).view(np.uint8)
    else:
        c = by_word.astype(ml_dtypes.float4_e2m1fn).view(np.uint8) & 0xF
        words = c[..., 0::2] | (c[..., 1::2] << 4)
    return np.ascontiguousarray(words), np.ascontiguousarray(byte.astype(np.uint8).reshape(k // 512, 16, n))


def unpack_weight(words, scales, fmt):
    g, p, n, _ = words.shape
    if fmt == "e4m3":
        vals = np.ascontiguousarray(words).view(ml_dtypes.float8_e4m3fn).astype(np.float64)
    else:
        nib = np.empty((g, p, n, 4), np.uint8)
        nib[..., 0::2] = words & 0xF
        nib[..., 1::2] = words >> 4
        vals = E2M1[nib]
    vals = vals * np.repeat(np.exp2(scales.astype(np.float64) - 127.0), 8, axis=1)[..., None]
    return vals.transpose(0, 1, 3, 2).reshape(g * 512, n)
def pack4(w):
    words, scales = pack_weight(w, "e2m1")
    return words.reshape(words.shape[0], 128, -1), scales


def unpack4(words, scales):
    return unpack_weight(words.reshape(words.shape[0], 128, -1, 2), scales, "e2m1")


B, T, C, H, NOPE, ROPE, VD, LORA = 1, 512, 2048, 16, 128, 128, 128, 512
EPS = 1e-6
HALF = ROPE // 2
KVW = H * (NOPE + VD)


def make_freq_cis():
    inv = 1.0 / (10000.0 ** (np.arange(0, ROPE, 2) / ROPE))
    ang = np.outer(np.arange(T), inv)
    return np.stack([np.cos(ang), np.sin(ang)], -1)


def apply_rope(v, fc):
    vr = v.reshape(B, T, HALF, 2)
    real = vr[..., 0] * fc[..., 0] - vr[..., 1] * fc[..., 1]
    imag = vr[..., 1] * fc[..., 0] + vr[..., 0] * fc[..., 1]
    return np.stack([real, imag], -1).reshape(B, T, ROPE)


def draw0():
    s, t = mx_kscale(C), mx_kscale(LORA)
    x = bf(np.random.standard_normal((B, T, C)) * s)
    freq_cis = bf(make_freq_cis())
    Wckv_words, Wckv_scales = pack4(np.random.standard_normal((C, LORA + ROPE)) / np.sqrt(C) / s[:, None])
    kv_norm_w = bf((1.0 + 0.1 * np.random.standard_normal(LORA)) * t)
    Wdkv_words, Wdkv_scales = pack4(np.random.standard_normal((LORA, KVW)) / np.sqrt(LORA) / t[:, None])
    return {"x": x,
            "freq_cis": freq_cis,
            "Wckv_words": Wckv_words,
            "Wckv_scales": Wckv_scales,
            "kv_norm_w": kv_norm_w,
            "Wdkv_words": Wdkv_words,
            "Wdkv_scales": Wdkv_scales}


def core(x, freq_cis, Wckv_words, Wckv_scales, kv_norm_w, Wdkv_words, Wdkv_scales):
    ckv = mxq(f64(x), 2, "e4m3") @ unpack4(Wckv_words, Wckv_scales)
    kv_lat, k_rope = ckv[..., :LORA], ckv[..., LORA:]
    k_rope = apply_rope(k_rope, f64(freq_cis))
    lat_n = kv_lat / np.sqrt(np.mean(kv_lat * kv_lat, -1, keepdims=True) + EPS) * f64(kv_norm_w)
    kv = mxq(lat_n, 2, "e4m3") @ unpack4(Wdkv_words, Wdkv_scales)
    return kv, k_rope


def e4m3fn_bytes(y):
    return np.clip(np.asarray(y, np.float64), -448.0, 448.0).astype(np.float32).astype(ml_dtypes.float8_e4m3fn).view(np.uint8)


def e4m3fn_values(b):
    return np.asarray(b, np.uint8).view(ml_dtypes.float8_e4m3fn).astype(np.float64)


def setup_inputs():
    d = draw0()
    x0 = np.asarray(d['x']).astype(np.float64)
    s = (np.max(np.abs(x0), axis=(0, 1), keepdims=True) / 448.0).astype(np.float32)
    out = {}
    for k, v in d.items():
        if k == 'x':
            out['x_bytes'] = e4m3fn_bytes(x0 / s.astype(np.float64))
            out['x_scale'] = s
        else:
            out[k] = v
    return out


def reference(x_bytes, x_scale, freq_cis, Wckv_words, Wckv_scales, kv_norm_w, Wdkv_words, Wdkv_scales):
    return core(e4m3fn_values(x_bytes) * x_scale.astype(np.float64), freq_cis, Wckv_words, Wckv_scales, kv_norm_w, Wdkv_words, Wdkv_scales)

@@ -1,0 +1,481 @@
+from contextlib import ExitStack
+
+import concourse.mybir as mybir
+from concourse.masks import make_identity
+
+F32 = mybir.dt.float32
+BF16 = mybir.dt.bfloat16
+U32 = mybir.dt.uint32
+U8 = mybir.dt.uint8
+I32 = mybir.dt.int32
+FP8 = mybir.dt.float8_e4m3fn
+FP8X4 = mybir.dt.float8_e4m3fn_x4
+FP4X4 = mybir.dt.float4_e2m1fn_x4
+ACT = mybir.ActivationFunctionType
+ALU = mybir.AluOpType
+
+P = 128
+T, C, LORA, ROPE, KVW = 512, 2048, 512, 128, 4096
+NT = T // P
+G = C // 512
+CKV = LORA + ROPE
+BANK = 512
+FLOPS = 2 * T * C * CKV + 2 * T * LORA * KVW
+EPS = 1e-6
+ORDER = [
+    ("w", 0, 2, 1),
+    ("T", 0, 2, 2),
+    ("w", 0, 1, 0),
+    ("w", 0, 3, 1),
+    ("T", 0, 3, 2),
+    ("w", 0, 0, 0),
+    ("T", 0, 1, 2),
+    ("p", 0, 2, 1),
+    ("p", 0, 3, 1),
+    ("T", 0, 0, 2),
+    ("p", 0, 1, 1),
+    ("w", 1, 1, 0),
+    ("w", 1, 0, 1),
+    ("T", 1, 0, 2),
+    ("T", 1, 1, 2),
+    ("p", 0, 0, 1),
+    ("w", 1, 3, 1),
+    ("w", 1, 2, 0),
+    ("gain", 0, 0, 0),
+    ("q", 0, 2, 1),
+    ("q", 0, 3, 1),
+    ("T", 1, 2, 2),
+    ("T", 1, 3, 2),
+    ("m", 0, 3, 2),
+    ("m", 0, 2, 2),
+    ("q", 0, 0, 1),
+    ("p", 1, 1, 1),
+    ("w", 2, 3, 0),
+    ("m", 0, 0, 2),
+    ("p", 1, 0, 1),
+    ("m", 0, 1, 2),
+    ("r", 0, 0, 2),
+    ("p", 1, 2, 1),
+    ("w", 2, 1, 0),
+    ("w", 2, 0, 0),
+    ("w", 2, 2, 0),
+    ("T", 2, 0, 2),
+    ("T", 2, 1, 2),
+    ("sq", 0, 0, 0),
+    ("sr", 0, 0, 0),
+    ("q", 1, 0, 1),
+    ("p", 1, 3, 1),
+    ("w", 3, 3, 0),
+    ("q", 1, 2, 1),
+    ("n", 0, 0, 1),
+    ("m", 1, 0, 2),
+    ("m", 1, 1, 2),
+    ("T", 2, 2, 2),
+    ("T", 2, 3, 2),
+    ("p", 2, 1, 1),
+    ("w", 3, 1, 0),
+    ("t", 0, 0, 2),
+    ("w", 3, 0, 0),
+    ("m", 1, 2, 2),
+    ("m", 1, 3, 2),
+    ("e", 0, 0, 0),
+    ("p", 2, 0, 1),
+    ("kc", 0, 0, 0),
+    ("w", 3, 2, 0),
+    ("T", 3, 0, 2),
+    ("T", 3, 1, 2),
+    ("z", 0, 0, 1),
+    ("p", 2, 3, 1),
+    ("sq", 1, 0, 0),
+    ("k", 0, 0, 2),
+    ("k", 0, 1, 2),
+    ("k", 0, 2, 2),
+    ("q", 2, 0, 1),
+    ("sr", 1, 0, 0),
+    ("c", 0, 0, 1),
+    ("o", 0, 0, 3),
+    ("k", 0, 3, 2),
+    ("m", 2, 0, 2),
+    ("m", 2, 1, 2),
+    ("c", 0, 1, 0),
+    ("o", 0, 4, 3),
+    ("n", 1, 0, 1),
+    ("k", 0, 4, 2),
+    ("c", 0, 2, 0),
+    ("p", 2, 2, 1),
+    ("k", 0, 5, 2),
+    ("c", 0, 3, 0),
+    ("o", 0, 1, 3),
+    ("t", 1, 0, 2),
+    ("T", 3, 2, 2),
+    ("T", 3, 3, 2),
+    ("k", 0, 6, 2),
+    ("c", 0, 4, 0),
+    ("p", 3, 1, 1),
+    ("q", 2, 2, 1),
+    ("e", 1, 0, 0),
+    ("k", 0, 7, 2),
+    ("c", 0, 5, 0),
+    ("o", 0, 2, 3),
+    ("m", 2, 2, 2),
+    ("m", 2, 3, 2),
+    ("c", 0, 6, 0),
+    ("p", 3, 0, 1),
+    ("z", 1, 0, 1),
+    ("c", 0, 7, 0),
+    ("o", 0, 3, 3),
+    ("p", 3, 3, 1),
+    ("sq", 2, 0, 0),
+    ("k", 1, 0, 2),
+    ("k", 1, 1, 2),
+    ("r", 1, 0, 2),
+    ("k", 1, 2, 2),
+    ("q", 3, 0, 1),
+    ("sr", 2, 0, 0),
+    ("c", 1, 0, 1),
+    ("kc", 1, 0, 0),
+    ("m", 3, 0, 2),
+    ("k", 1, 3, 2),
+    ("m", 3, 1, 2),
+    ("c", 1, 1, 1),
+    ("o", 1, 0, 3),
+    ("n", 2, 0, 1),
+    ("k", 1, 4, 2),
+    ("c", 1, 2, 0),
+    ("p", 3, 2, 1),
+    ("k", 1, 5, 2),
+    ("c", 1, 3, 0),
+    ("o", 1, 1, 3),
+    ("t", 2, 0, 2),
+    ("k", 1, 6, 2),
+    ("c", 1, 4, 0),
+    ("q", 3, 2, 1),
+    ("e", 2, 0, 0),
+    ("k", 1, 7, 2),
+    ("c", 1, 5, 1),
+    ("o", 1, 2, 3),
+    ("m", 3, 2, 2),
+    ("m", 3, 3, 2),
+    ("c", 1, 6, 0),
+    ("z", 2, 0, 1),
+    ("c", 1, 7, 0),
+    ("o", 1, 3, 3),
+    ("sq", 3, 0, 0),
+    ("k", 2, 0, 2),
+    ("k", 2, 1, 2),
+    ("r", 2, 0, 2),
+    ("k", 2, 2, 2),
+    ("sr", 3, 0, 0),
+    ("c", 2, 0, 1),
+    ("kc", 2, 0, 0),
+    ("k", 2, 3, 2),
+    ("c", 2, 1, 1),
+    ("o", 2, 0, 3),
+    ("n", 3, 0, 1),
+    ("k", 2, 4, 2),
+    ("c", 2, 2, 0),
+    ("k", 2, 5, 2),
+    ("c", 2, 3, 0),
+    ("o", 2, 1, 3),
+    ("t", 3, 0, 2),
+    ("k", 2, 6, 2),
+    ("c", 2, 4, 0),
+    ("e", 3, 0, 0),
+    ("k", 2, 7, 2),
+    ("c", 2, 5, 1),
+    ("o", 2, 2, 3),
+    ("c", 2, 6, 0),
+    ("z", 3, 0, 1),
+    ("c", 2, 7, 0),
+    ("o", 2, 3, 3),
+    ("k", 3, 0, 2),
+    ("k", 3, 1, 2),
+    ("r", 3, 0, 2),
+    ("k", 3, 2, 2),
+    ("c", 3, 0, 1),
+    ("kc", 3, 0, 0),
+    ("k", 3, 3, 2),
+    ("c", 3, 1, 1),
+    ("o", 3, 0, 3),
+    ("k", 3, 4, 2),
+    ("c", 3, 2, 0),
+    ("k", 3, 5, 2),
+    ("c", 3, 3, 0),
+    ("o", 3, 1, 3),
+    ("k", 3, 6, 2),
+    ("c", 3, 4, 0),
+    ("k", 3, 7, 2),
+    ("c", 3, 5, 1),
+    ("o", 3, 2, 3),
+    ("c", 3, 6, 0),
+    ("o", 3, 3, 3),
+    ("c", 3, 7, 0),
+    ("o", 3, 4, 3),
+]
+
+
+def tile_multiheadlatentattention_pa_w4_kernel(
+    tc, x_bytes, x_scale, freq_cis, Wckv_words, Wckv_scales, kv_norm_w, Wdkv_words, Wdkv_scales, out_0, out_1
+):
+    nc = tc.nc
+    with ExitStack() as ctx:
+        keep = ctx.enter_context(tc.tile_pool(name="keep", bufs=1))
+        work = ctx.enter_context(tc.tile_pool(name="work", bufs=4))
+        outs = ctx.enter_context(tc.tile_pool(name="outs", bufs=16))
+        ps_x = ctx.enter_context(tc.psum_pool(name="ps_x", bufs=2))
+        ps_l = ctx.enter_context(tc.psum_pool(name="ps_l", bufs=2))
+        ps_k = ctx.enter_context(tc.psum_pool(name="ps_k", bufs=4))
+
+        xb = keep.tile([P, NT, C], U8, name="xb", align_bytes=64)
+        sc = keep.tile([P, G, 8], F32, name="sc", align_bytes=64)
+        wa = keep.tile([P, G, 2 * CKV], U8, name="wa", align_bytes=64)
+        wa_s = keep.tile([P, G, CKV], U8, name="wa_s", align_bytes=64)
+        wb = keep.tile([P, 2 * KVW], U8, name="wb", align_bytes=64)
+        wb_s = keep.tile([P, KVW], U8, name="wb_s", align_bytes=64)
+        fr = keep.tile([P, NT, ROPE // 2, 2], BF16, name="fr")
+        ident = keep.tile([P, P], F32, name="ident")
+        row = keep.tile([P, LORA], BF16, name="row")
+        ones = keep.tile([P, BANK], BF16, name="ones")
+        gain = keep.tile([P, LORA], BF16, name="gain")
+        ss = keep.tile([P, NT], F32, name="ss")
+        rs = keep.tile([P, NT], F32, name="rs")
+        krs = keep.tile([P, NT, ROPE], F32, name="krs")
+        dummy = keep.tile([P, 1], F32, name="dummy")
+
+        wa_s32 = wa_s[:].rearrange("p g n -> p (g n)").bitcast(I32)
+        nc.gpsimd.memset(wa_s32, 0)
+        nc.vector.memset(dummy[:], 1.0)
+        nc.vector.memset(ones[:], 1.0)
+        nc.vector.memset(wb_s[:].bitcast(I32), 0)
+        nc.vector.memset(row[:], 0.0)
+        nc.scalar.activation(out=dummy[:], in_=dummy[:], func=ACT.Abs_reciprocal_sqrt)
+
+        def load_x(i, c0, c1):
+            nc.sync.dma_start(out=xb[:, i, c0:c1], in_=x_bytes[0, i * P : (i + 1) * P, c0:c1])
+
+        load_x(0, 0, 1024)
+        load_x(0, 1024, 2048)
+        nc.sync.dma_start(out=sc[:, :, 0:4], in_=x_scale.rearrange("a b (g p t) -> p (a b g) t", p=P, t=4))
+        wa_s3 = wa_s32.rearrange("p (g n) -> p g n", g=G)
+        src = Wckv_scales.bitcast(I32).rearrange("g (q r) n -> r q g n", r=4)
+        for r in range(4):
+            nc.sync.dma_start(out=wa_s3[r:P:32], in_=src[r])
+        nc.sync.dma_start(out=wa[:], in_=Wckv_words.rearrange("g p c -> p g c"))
+        make_identity(nc, ident[:])
+        load_x(1, 0, 2048)
+        nc.gpsimd.dma_start(out=row[0:1, :], in_=kv_norm_w.rearrange("(o n) -> o n", o=1))
+        nc.gpsimd.dma_start(out=fr[:], in_=freq_cis.rearrange("(i p) h c -> p i h c", p=P))
+        load_x(2, 0, 2048)
+        src = Wdkv_scales.bitcast(I32).rearrange("g (q r) n -> r (g q) n", r=4)
+        for r in range(4):
+            nc.sync.dma_start(out=wb_s[:].bitcast(I32)[r:P:32], in_=src[r])
+        for h in range(2):
+            nc.sync.dma_start(out=wb[:, h * KVW : (h + 1) * KVW], in_=Wdkv_words[0, :, h * KVW : (h + 1) * KVW])
+        load_x(3, 0, 2048)
+
+        def warm(n):
+            hot = ps_k.tile([P, BANK], F32, name="kvb")
+            for _ in range(n):
+                nc.tensor.matmul(hot[:], lhsT=ones[:, 0:P], rhs=ones[:], start=True, stop=True)
+
+        xw, xg, xt, codes, scales, lat, nb, nt, ng, ncodes, nscales, kr, kv, ob = ({} for _ in range(14))
+
+        def do_gain():
+            gp = ps_k.tile([P, BANK], F32, name="kvb")
+            nc.tensor.matmul(gp[:], lhsT=ones[:, 0:P], rhs=row[:], start=True, stop=True)
+            nc.scalar.copy(out=gain[:], in_=gp[:])
+
+        def do_w(i, g, eng):
+            if i not in xw:
+                xw[i] = work.tile([P, C], BF16, name="xwt")
+            c = slice(512 * g, 512 * (g + 1))
+            src = xb[:, i, c].bitcast(FP8)
+            if eng == 0:
+                nc.scalar.copy(out=xw[i][:, c], in_=src)
+            else:
+                nc.vector.tensor_copy(out=xw[i][:, c], in_=src)
+
+        def do_T(i, g):
+            if i == 0:
+                if g < 2:
+                    bank = ps_x.tile([P, BANK], F32, name="xtb")
+                else:
+                    bank = ps_k.tile([P, BANK], F32, name="kvb")
+                xt[i, g] = bank[:, 0:256]
+            elif (i, g) not in xt:
+                bank = ps_x.tile([P, BANK], F32, name="xtb")
+                for k in range(2):
+                    xt[i, (g & 2) + k] = bank[:, 256 * k : 256 * (k + 1)]
+            words = xw[i][:].bitcast(F32)
+            for u in range(2):
+                nc.tensor.transpose(xt[i, g][:, P * u : P * (u + 1)], words[:, 256 * g + u : 256 * (g + 1) : 2], ident[:])
+
+        def do_p(i, g, eng):
+            if i not in xg:
+                xg[i] = work.tile([P, G, P, 4], BF16, name="xgt", align_bytes=64)
+            if eng == 0:
+                for u in range(2):
+                    for e in range(2):
+                        nc.scalar.activation(
+                            out=xg[i][:, g, :, 2 * u + e : 2 * u + e + 1],
+                            in_=xt[i, g].bitcast(BF16).rearrange("p (u r e) -> p u r e", u=2, e=2)[:, u, :, e : e + 1],
+                            func=ACT.Copy,
+                            scale=sc[:, g, 2 * u + e : 2 * u + e + 1],
+                        )
+                return
+            nc.vector.tensor_tensor(
+                out=xg[i][:, g].rearrange("p r (u e) -> p r u e", e=2),
+                in0=xt[i, g].bitcast(BF16).rearrange("p (u r e) -> p r u e", u=2, e=2),
+                in1=sc[:, g : g + 1, 0:4].rearrange("p o (u e) -> p o u e", e=2).to_broadcast([P, P, 2, 2]),
+                op=ALU.mult,
+            )
+
+        def do_q(i, g):
+            if i not in codes:
+                codes[i] = work.tile([P, G, P], U32, name="codest", align_bytes=64)
+                scales[i] = work.tile([P, G, P], U8, name="scalest", align_bytes=64)
+            n = 1 if i == 0 and g >= 2 else 2
+            gs = slice(g, g + n)
+            nc.vector.quantize_mx(
+                out=codes[i][:, gs].rearrange("p g r -> p (g r)").bitcast(FP8X4),
+                scales=scales[i][:, gs].rearrange("p g r -> p (g r)"),
+                in_=xg[i][:, gs].rearrange("p g r t -> p (g r t)"),
+            )
+
+        order_m = {}
+
+        def mm1(i, g, dst, c0, n, start, stop):
+            nc.tensor.matmul_mx(
+                out=dst,
+                lhsT=codes[i][:, g].bitcast(FP8X4),
+                lhsT_scale=scales[i][:, g],
+                rhs=wa[:, g, 2 * c0 : 2 * (c0 + n)].bitcast(FP4X4),
+                rhs_scale=wa_s[:, g, c0 : c0 + n],
+                start=start,
+                stop=stop,
+            )
+
+        def do_m(i, g):
+            if i not in lat:
+                lat[i] = ps_l.tile([P, LORA], F32, name="latt")
+                order_m[i] = 0
+            mm1(i, g, lat[i][:], 0, LORA, order_m[i] == 0, order_m[i] == G - 1)
+            order_m[i] += 1
+
+        def do_r(i):
+            kr[i] = ps_k.tile([P, BANK], F32, name="kvb")
+            for g in range(G):
+                mm1(i, g, kr[i][:, 0:ROPE], LORA, ROPE, g == 0, g == G - 1)
+
+        def do_kc(i):
+            nc.scalar.copy(out=krs[:, i], in_=kr[i][:, 0:ROPE])
+
+        def do_sq(i):
+            junk = work.tile([P, LORA], F32, name="junk")
+            nc.scalar.activation(out=junk[:], in_=lat[i][:], func=ACT.Square, accum_out=ss[:, i : i + 1])
+
+        def do_sr(i):
+            nc.scalar.activation(
+                out=rs[:, i : i + 1], in_=ss[:, i : i + 1], func=ACT.Abs_reciprocal_sqrt, scale=1.0 / LORA, bias=EPS
+            )
+
+        def do_n(i):
+            nb[i] = work.tile([P, LORA], BF16, name="nbt")
+            nc.vector.scalar_tensor_tensor(
+                out=nb[i][:], in0=lat[i][:], scalar=rs[:, i : i + 1], in1=gain[:], op0=ALU.mult, op1=ALU.mult
+            )
+
+        def do_t(i):
+            nt[i] = ps_k.tile([P, BANK], F32, name="kvb")
+            words = nb[i][:].bitcast(F32)
+            for u in range(2):
+                nc.tensor.transpose(nt[i][:, P * u : P * (u + 1)], words[:, u:256:2], ident[:])
+
+        def do_e(i):
+            ng[i] = work.tile([P, 4 * P], BF16, name="ngt", align_bytes=64)
+            nc.scalar.copy(
+                out=ng[i][:].bitcast(F32).rearrange("p (r u) -> p r u", u=2),
+                in_=nt[i][:, 0:256].rearrange("p (u r) -> p r u", u=2),
+            )
+
+        def do_z(i):
+            ncodes[i] = work.tile([P, P], U32, name="ncodest", align_bytes=64)
+            nscales[i] = work.tile([P, P], U8, name="nscalest", align_bytes=64)
+            nc.vector.quantize_mx(out=ncodes[i][:].bitcast(FP8X4), scales=nscales[i][:], in_=ng[i][:])
+
+        def do_k(i, j):
+            kv[i, j] = ps_k.tile([P, BANK], F32, name="kvb")
+            nc.tensor.matmul_mx(
+                out=kv[i, j][:],
+                lhsT=ncodes[i][:].bitcast(FP8X4),
+                lhsT_scale=nscales[i][:],
+                rhs=wb[:, 2 * BANK * j : 2 * BANK * (j + 1)].bitcast(FP4X4),
+                rhs_scale=wb_s[:, BANK * j : BANK * (j + 1)],
+                start=True,
+                stop=True,
+            )
+
+        def do_c(i, j, eng):
+            h, k = divmod(j, 2)
+            if (i, h) not in ob:
+                ob[i, h] = outs.tile([P, 2, BANK], F32, name="obt")
+            if eng == 1:
+                nc.vector.tensor_copy(out=ob[i, h][:, k], in_=kv[i, j][:])
+            else:
+                nc.scalar.copy(out=ob[i, h][:, k], in_=kv[i, j][:])
+
+        def do_o(i, h):
+            rows = slice(i * P, (i + 1) * P)
+            b, lo, hi = h, 0, 2
+            if (i, h) == (0, 0):
+                hi = 1
+            elif (i, h) == (0, 4):
+                b, lo = 0, 1
+            elif (i, h) == (3, 3):
+                hi = 1
+            elif (i, h) == (3, 4):
+                b, lo = 3, 1
+            nc.sync.dma_start(
+                out=out_0[0, rows, BANK * (2 * b + lo) : BANK * (2 * b + hi)],
+                in_=ob[i, b][:, lo:hi].rearrange("p k n -> p (k n)"),
+            )
+
+        def do_rope(i0, i1):
+            n = (i1 - i0) * (ROPE // 2)
+            a, b, o = (work.tile([P, NT, ROPE], F32, name=nm) for nm in ("ra", "rb", "ro"))
+            a2, b2, o2, k2 = (
+                v[:, i0:i1].rearrange("p i (h e) -> p (i h) e", e=2) for v in (a[:], b[:], o[:], krs[:])
+            )
+            f2 = fr[:, i0:i1].rearrange("p i h e -> p (i h) e")
+            shape = [P, n, 2]
+            nc.gpsimd.tensor_tensor(out=a2, in0=k2, in1=f2[:, :, 0:1].to_broadcast(shape), op=ALU.mult)
+            nc.gpsimd.tensor_tensor(out=b2, in0=k2, in1=f2[:, :, 1:2].to_broadcast(shape), op=ALU.mult)
+            nc.gpsimd.tensor_tensor(out=o2[:, :, 0:1], in0=a2[:, :, 0:1], in1=b2[:, :, 1:2], op=ALU.subtract)
+            nc.gpsimd.tensor_tensor(out=o2[:, :, 1:2], in0=a2[:, :, 1:2], in1=b2[:, :, 0:1], op=ALU.add)
+            return i0, i1, o
+
+        def do_rope_store(i0, i1, o):
+            nc.sync.dma_start(
+                out=out_1[0, i0 * P : i1 * P, :].rearrange("(i p) c -> p i c", p=P), in_=o[:, i0:i1]
+            )
+
+        table = {
+            "w": do_w, "T": do_T, "p": do_p, "q": do_q, "m": do_m, "r": do_r, "kc": do_kc, "sq": do_sq, "sr": do_sr,
+            "n": do_n, "t": do_t, "e": do_e, "z": do_z, "k": do_k, "c": do_c, "o": do_o,
+        }
+        rotated = []
+        with tc.manual_schedule():
+            warm(3)
+            for kind, i, j, eng in ORDER:
+                if kind == "gain":
+                    do_gain()
+                elif kind in ("w", "c", "p"):
+                    table[kind](i, j, eng)
+                elif kind in ("T", "q", "m", "k", "o"):
+                    table[kind](i, j)
+                else:
+                    table[kind](i)
+                if (kind, i) in (("kc", 1), ("kc", 3)):
+                    rotated.append(do_rope(i - 1, i + 1))
+                if (kind, i, j) in (("o", 2, 0), ("o", 3, 2)):
+                    do_rope_store(*rotated.pop())

@@ -22,152 +22,155 @@ CKV = LORA + ROPE
 BANK = 512
 FLOPS = 2 * T * C * CKV + 2 * T * LORA * KVW
 EPS = 1e-6
+LAST_T0 = 1
+WARM = (3, 2)
+STORE_ROPE = {("o", 1, 1): 1, ("o", 3, 0): 3}
 ORDER = [
-    ("w", 0, 2, 1),
-    ("T", 0, 2, 2),
-    ("w", 0, 1, 0),
     ("w", 0, 3, 1),
+    ("w", 0, 0, 1),
+    ("w", 0, 2, 0),
     ("T", 0, 3, 2),
-    ("w", 0, 0, 0),
-    ("T", 0, 1, 2),
-    ("p", 0, 2, 1),
-    ("p", 0, 3, 1),
+    ("w", 0, 1, 0),
     ("T", 0, 0, 2),
-    ("p", 0, 1, 1),
-    ("w", 1, 1, 0),
-    ("w", 1, 0, 1),
-    ("T", 1, 0, 2),
-    ("T", 1, 1, 2),
+    ("p", 0, 3, 1),
     ("p", 0, 0, 1),
+    ("q", 0, 3, 1),
+    ("T", 0, 2, 2),
+    ("p", 0, 2, 1),
+    ("T", 0, 1, 2),
+    ("gain", 0, 0, 0),
+    ("w", 1, 1, 1),
+    ("p", 0, 1, 1),
+    ("w", 1, 0, 0),
+    ("m", 0, 3, 2),
     ("w", 1, 3, 1),
     ("w", 1, 2, 0),
-    ("gain", 0, 0, 0),
+    ("T", 1, 0, 2),
+    ("T", 1, 1, 2),
     ("q", 0, 2, 1),
-    ("q", 0, 3, 1),
+    ("q", 0, 0, 1),
     ("T", 1, 2, 2),
     ("T", 1, 3, 2),
-    ("m", 0, 3, 2),
     ("m", 0, 2, 2),
-    ("q", 0, 0, 1),
-    ("p", 1, 1, 1),
-    ("w", 2, 3, 0),
     ("m", 0, 0, 2),
-    ("p", 1, 0, 1),
     ("m", 0, 1, 2),
-    ("r", 0, 0, 2),
+    ("p", 1, 0, 1),
+    ("w", 2, 3, 0),
+    ("p", 1, 1, 1),
+    ("p", 1, 3, 1),
     ("p", 1, 2, 1),
+    ("q", 1, 0, 1),
     ("w", 2, 1, 0),
     ("w", 2, 0, 0),
-    ("w", 2, 2, 0),
+    ("r", 0, 0, 2),
     ("T", 2, 0, 2),
     ("T", 2, 1, 2),
+    ("w", 2, 2, 0),
+    ("q", 1, 2, 1),
     ("sq", 0, 0, 0),
     ("sr", 0, 0, 0),
-    ("q", 1, 0, 1),
-    ("p", 1, 3, 1),
-    ("w", 3, 3, 0),
-    ("q", 1, 2, 1),
     ("n", 0, 0, 1),
-    ("m", 1, 0, 2),
-    ("m", 1, 1, 2),
+    ("w", 3, 3, 0),
     ("T", 2, 2, 2),
     ("T", 2, 3, 2),
-    ("p", 2, 1, 1),
     ("w", 3, 1, 0),
+    ("m", 1, 0, 2),
+    ("m", 1, 1, 2),
     ("t", 0, 0, 2),
     ("w", 3, 0, 0),
+    ("p", 2, 1, 1),
+    ("p", 2, 0, 1),
+    ("p", 2, 3, 1),
+    ("e", 0, 0, 0),
+    ("z", 0, 0, 1),
     ("m", 1, 2, 2),
     ("m", 1, 3, 2),
-    ("e", 0, 0, 0),
-    ("p", 2, 0, 1),
-    ("kc", 0, 0, 0),
-    ("w", 3, 2, 0),
     ("T", 3, 0, 2),
     ("T", 3, 1, 2),
-    ("z", 0, 0, 1),
-    ("p", 2, 3, 1),
-    ("sq", 1, 0, 0),
+    ("w", 3, 2, 0),
+    ("q", 2, 0, 1),
+    ("kc", 0, 0, 1),
     ("k", 0, 0, 2),
+    ("p", 2, 2, 1),
     ("k", 0, 1, 2),
     ("k", 0, 2, 2),
-    ("q", 2, 0, 1),
-    ("sr", 1, 0, 0),
-    ("c", 0, 0, 1),
-    ("o", 0, 0, 3),
-    ("k", 0, 3, 2),
+    ("sq", 1, 0, 0),
     ("m", 2, 0, 2),
     ("m", 2, 1, 2),
+    ("sr", 1, 0, 0),
+    ("c", 0, 0, 0),
+    ("o", 0, 0, 3),
+    ("k", 0, 3, 2),
     ("c", 0, 1, 0),
     ("o", 0, 4, 3),
     ("n", 1, 0, 1),
     ("k", 0, 4, 2),
-    ("c", 0, 2, 0),
-    ("p", 2, 2, 1),
-    ("k", 0, 5, 2),
-    ("c", 0, 3, 0),
-    ("o", 0, 1, 3),
-    ("t", 1, 0, 2),
     ("T", 3, 2, 2),
     ("T", 3, 3, 2),
-    ("k", 0, 6, 2),
-    ("c", 0, 4, 0),
-    ("p", 3, 1, 1),
+    ("c", 0, 2, 0),
+    ("t", 1, 0, 2),
+    ("k", 0, 5, 2),
     ("q", 2, 2, 1),
-    ("e", 1, 0, 0),
+    ("c", 0, 3, 0),
+    ("o", 0, 1, 3),
+    ("k", 0, 6, 2),
+    ("p", 3, 1, 1),
+    ("p", 3, 0, 1),
+    ("c", 0, 4, 0),
+    ("p", 3, 3, 1),
     ("k", 0, 7, 2),
+    ("e", 1, 0, 0),
     ("c", 0, 5, 0),
     ("o", 0, 2, 3),
+    ("q", 3, 0, 1),
     ("m", 2, 2, 2),
     ("m", 2, 3, 2),
-    ("c", 0, 6, 0),
-    ("p", 3, 0, 1),
+    ("r", 1, 0, 2),
     ("z", 1, 0, 1),
+    ("c", 0, 6, 1),
+    ("k", 1, 0, 2),
+    ("p", 3, 2, 1),
     ("c", 0, 7, 0),
     ("o", 0, 3, 3),
-    ("p", 3, 3, 1),
-    ("sq", 2, 0, 0),
-    ("k", 1, 0, 2),
     ("k", 1, 1, 2),
-    ("r", 1, 0, 2),
+    ("kc", 1, 0, 1),
     ("k", 1, 2, 2),
-    ("q", 3, 0, 1),
-    ("sr", 2, 0, 0),
-    ("c", 1, 0, 1),
-    ("kc", 1, 0, 0),
+    ("sq", 2, 0, 0),
     ("m", 3, 0, 2),
-    ("k", 1, 3, 2),
     ("m", 3, 1, 2),
+    ("c", 1, 0, 0),
+    ("sr", 2, 0, 0),
+    ("k", 1, 3, 2),
     ("c", 1, 1, 1),
     ("o", 1, 0, 3),
     ("n", 2, 0, 1),
     ("k", 1, 4, 2),
     ("c", 1, 2, 0),
-    ("p", 3, 2, 1),
     ("k", 1, 5, 2),
+    ("t", 2, 0, 2),
+    ("q", 3, 2, 1),
     ("c", 1, 3, 0),
     ("o", 1, 1, 3),
-    ("t", 2, 0, 2),
     ("k", 1, 6, 2),
-    ("c", 1, 4, 0),
-    ("q", 3, 2, 1),
-    ("e", 2, 0, 0),
+    ("c", 1, 4, 1),
     ("k", 1, 7, 2),
-    ("c", 1, 5, 1),
+    ("c", 1, 5, 0),
     ("o", 1, 2, 3),
+    ("e", 2, 0, 0),
     ("m", 3, 2, 2),
     ("m", 3, 3, 2),
-    ("c", 1, 6, 0),
-    ("z", 2, 0, 1),
-    ("c", 1, 7, 0),
-    ("o", 1, 3, 3),
-    ("sq", 3, 0, 0),
-    ("k", 2, 0, 2),
-    ("k", 2, 1, 2),
     ("r", 2, 0, 2),
+    ("z", 2, 0, 1),
+    ("c", 1, 6, 0),
+    ("k", 2, 0, 2),
+    ("c", 1, 7, 1),
+    ("o", 1, 3, 3),
+    ("k", 2, 1, 2),
+    ("kc", 2, 0, 1),
     ("k", 2, 2, 2),
+    ("sq", 3, 0, 0),
+    ("c", 2, 0, 0),
     ("sr", 3, 0, 0),
-    ("c", 2, 0, 1),
-    ("kc", 2, 0, 0),
     ("k", 2, 3, 2),
     ("c", 2, 1, 1),
     ("o", 2, 0, 3),
@@ -175,25 +178,25 @@ ORDER = [
     ("k", 2, 4, 2),
     ("c", 2, 2, 0),
     ("k", 2, 5, 2),
+    ("t", 3, 0, 2),
     ("c", 2, 3, 0),
     ("o", 2, 1, 3),
-    ("t", 3, 0, 2),
     ("k", 2, 6, 2),
-    ("c", 2, 4, 0),
-    ("e", 3, 0, 0),
+    ("c", 2, 4, 1),
     ("k", 2, 7, 2),
-    ("c", 2, 5, 1),
+    ("c", 2, 5, 0),
     ("o", 2, 2, 3),
-    ("c", 2, 6, 0),
-    ("z", 3, 0, 1),
-    ("c", 2, 7, 0),
-    ("o", 2, 3, 3),
-    ("k", 3, 0, 2),
-    ("k", 3, 1, 2),
+    ("e", 3, 0, 0),
     ("r", 3, 0, 2),
+    ("z", 3, 0, 1),
+    ("c", 2, 6, 0),
+    ("k", 3, 0, 2),
+    ("c", 2, 7, 1),
+    ("o", 2, 3, 3),
+    ("k", 3, 1, 2),
+    ("kc", 3, 0, 1),
     ("k", 3, 2, 2),
-    ("c", 3, 0, 1),
-    ("kc", 3, 0, 0),
+    ("c", 3, 0, 0),
     ("k", 3, 3, 2),
     ("c", 3, 1, 1),
     ("o", 3, 0, 3),
@@ -203,13 +206,13 @@ ORDER = [
     ("c", 3, 3, 0),
     ("o", 3, 1, 3),
     ("k", 3, 6, 2),
-    ("c", 3, 4, 0),
+    ("c", 3, 4, 1),
     ("k", 3, 7, 2),
-    ("c", 3, 5, 1),
+    ("c", 3, 5, 0),
     ("o", 3, 2, 3),
     ("c", 3, 6, 0),
     ("o", 3, 3, 3),
-    ("c", 3, 7, 0),
+    ("c", 3, 7, 1),
     ("o", 3, 4, 3),
 ]
 
@@ -239,31 +242,32 @@ def tile_multiheadlatentattention_pa_w4_kernel(
         gain = keep.tile([P, LORA], BF16, name="gain")
         ss = keep.tile([P, NT], F32, name="ss")
         rs = keep.tile([P, NT], F32, name="rs")
-        krs = keep.tile([P, NT, ROPE], F32, name="krs")
+        ra = keep.tile([P, NT, ROPE], F32, name="ra")
+        rb = keep.tile([P, NT, ROPE], F32, name="rb")
+        ro = keep.tile([P, NT, ROPE], F32, name="ro")
         dummy = keep.tile([P, 1], F32, name="dummy")
 
         wa_s32 = wa_s[:].rearrange("p g n -> p (g n)").bitcast(I32)
-        nc.gpsimd.memset(wa_s32, 0)
-        nc.vector.memset(dummy[:], 1.0)
-        nc.vector.memset(ones[:], 1.0)
-        nc.vector.memset(wb_s[:].bitcast(I32), 0)
+        make_identity(nc, ident[:])
         nc.vector.memset(row[:], 0.0)
+        nc.scalar.dma_start(out=row[0:1, :], in_=kv_norm_w.rearrange("(o n) -> o n", o=1))
+        nc.vector.memset(wa_s32, 0)
+        nc.vector.memset(ones[:], 1.0)
+        nc.vector.memset(dummy[:], 1.0)
+        nc.vector.memset(wb_s[:].bitcast(I32), 0)
         nc.scalar.activation(out=dummy[:], in_=dummy[:], func=ACT.Abs_reciprocal_sqrt)
 
         def load_x(i, c0, c1):
             nc.sync.dma_start(out=xb[:, i, c0:c1], in_=x_bytes[0, i * P : (i + 1) * P, c0:c1])
 
-        load_x(0, 0, 1024)
-        load_x(0, 1024, 2048)
+        load_x(0, 0, 2048)
         nc.sync.dma_start(out=sc[:, :, 0:4], in_=x_scale.rearrange("a b (g p t) -> p (a b g) t", p=P, t=4))
         wa_s3 = wa_s32.rearrange("p (g n) -> p g n", g=G)
         src = Wckv_scales.bitcast(I32).rearrange("g (q r) n -> r q g n", r=4)
         for r in range(4):
             nc.sync.dma_start(out=wa_s3[r:P:32], in_=src[r])
         nc.sync.dma_start(out=wa[:], in_=Wckv_words.rearrange("g p c -> p g c"))
-        make_identity(nc, ident[:])
         load_x(1, 0, 2048)
-        nc.gpsimd.dma_start(out=row[0:1, :], in_=kv_norm_w.rearrange("(o n) -> o n", o=1))
         nc.gpsimd.dma_start(out=fr[:], in_=freq_cis.rearrange("(i p) h c -> p i h c", p=P))
         load_x(2, 0, 2048)
         src = Wdkv_scales.bitcast(I32).rearrange("g (q r) n -> r (g q) n", r=4)
@@ -280,10 +284,13 @@ def tile_multiheadlatentattention_pa_w4_kernel(
 
         xw, xg, xt, codes, scales, lat, nb, nt, ng, ncodes, nscales, kr, kv, ob = ({} for _ in range(14))
 
-        def do_gain():
-            gp = ps_k.tile([P, BANK], F32, name="kvb")
-            nc.tensor.matmul(gp[:], lhsT=ones[:, 0:P], rhs=row[:], start=True, stop=True)
-            nc.scalar.copy(out=gain[:], in_=gp[:])
+        def gain_matmul():
+            bank = ps_k.tile([P, BANK], F32, name="kvb")
+            nc.tensor.matmul(bank[:], lhsT=ones[:, 0:P], rhs=row[:], start=True, stop=True)
+            return bank
+
+        def do_gain(bank):
+            nc.scalar.copy(out=gain[:], in_=bank[:])
 
         def do_w(i, g, eng):
             if i not in xw:
@@ -368,7 +375,24 @@ def tile_multiheadlatentattention_pa_w4_kernel(
                 mm1(i, g, kr[i][:, 0:ROPE], LORA, ROPE, g == 0, g == G - 1)
 
         def do_kc(i):
-            nc.scalar.copy(out=krs[:, i], in_=kr[i][:, 0:ROPE])
+            shape = [P, ROPE // 2, 2]
+            pairs = kr[i][:, 0:ROPE].rearrange("p (h e) -> p h e", e=2)
+            for dst, c in ((ra, 0), (rb, 1)):
+                nc.vector.tensor_tensor(
+                    out=dst[:, i].rearrange("p (h e) -> p h e", e=2),
+                    in0=pairs,
+                    in1=fr[:, i, :, c : c + 1].to_broadcast(shape),
+                    op=ALU.mult,
+                )
+            if i % 2:
+                a2, b2, o2 = (v[:, i - 1 : i + 1].rearrange("p i (h e) -> p (i h) e", e=2) for v in (ra, rb, ro))
+                nc.vector.tensor_tensor(out=o2[:, :, 0:1], in0=a2[:, :, 0:1], in1=b2[:, :, 1:2], op=ALU.subtract)
+                nc.vector.tensor_tensor(out=o2[:, :, 1:2], in0=a2[:, :, 1:2], in1=b2[:, :, 0:1], op=ALU.add)
+
+        def do_rope_store(i):
+            nc.sync.dma_start(
+                out=out_1[0, (i - 1) * P : (i + 1) * P, :].rearrange("(i p) c -> p i c", p=P), in_=ro[:, i - 1 : i + 1]
+            )
 
         def do_sq(i):
             junk = work.tile([P, LORA], F32, name="junk")
@@ -440,42 +464,24 @@ def tile_multiheadlatentattention_pa_w4_kernel(
                 in_=ob[i, b][:, lo:hi].rearrange("p k n -> p (k n)"),
             )
 
-        def do_rope(i0, i1):
-            n = (i1 - i0) * (ROPE // 2)
-            a, b, o = (work.tile([P, NT, ROPE], F32, name=nm) for nm in ("ra", "rb", "ro"))
-            a2, b2, o2, k2 = (
-                v[:, i0:i1].rearrange("p i (h e) -> p (i h) e", e=2) for v in (a[:], b[:], o[:], krs[:])
-            )
-            f2 = fr[:, i0:i1].rearrange("p i h e -> p (i h) e")
-            shape = [P, n, 2]
-            nc.gpsimd.tensor_tensor(out=a2, in0=k2, in1=f2[:, :, 0:1].to_broadcast(shape), op=ALU.mult)
-            nc.gpsimd.tensor_tensor(out=b2, in0=k2, in1=f2[:, :, 1:2].to_broadcast(shape), op=ALU.mult)
-            nc.gpsimd.tensor_tensor(out=o2[:, :, 0:1], in0=a2[:, :, 0:1], in1=b2[:, :, 1:2], op=ALU.subtract)
-            nc.gpsimd.tensor_tensor(out=o2[:, :, 1:2], in0=a2[:, :, 1:2], in1=b2[:, :, 0:1], op=ALU.add)
-            return i0, i1, o
-
-        def do_rope_store(i0, i1, o):
-            nc.sync.dma_start(
-                out=out_1[0, i0 * P : i1 * P, :].rearrange("(i p) c -> p i c", p=P), in_=o[:, i0:i1]
-            )
-
         table = {
             "w": do_w, "T": do_T, "p": do_p, "q": do_q, "m": do_m, "r": do_r, "kc": do_kc, "sq": do_sq, "sr": do_sr,
             "n": do_n, "t": do_t, "e": do_e, "z": do_z, "k": do_k, "c": do_c, "o": do_o,
         }
-        rotated = []
         with tc.manual_schedule():
-            warm(3)
+            warm(WARM[0])
             for kind, i, j, eng in ORDER:
                 if kind == "gain":
-                    do_gain()
+                    do_gain(gain_bank)
                 elif kind in ("w", "c", "p"):
                     table[kind](i, j, eng)
                 elif kind in ("T", "q", "m", "k", "o"):
                     table[kind](i, j)
                 else:
                     table[kind](i)
-                if (kind, i) in (("kc", 1), ("kc", 3)):
-                    rotated.append(do_rope(i - 1, i + 1))
-                if (kind, i, j) in (("o", 2, 0), ("o", 3, 2)):
-                    do_rope_store(*rotated.pop())
+                if kind == "T" and len(xt) == 1:
+                    gain_bank = gain_matmul()
+                if (kind, i, j) == ("T", 0, LAST_T0):
+                    warm(WARM[1])
+                if (kind, i, j) in STORE_ROPE:
+                    do_rope_store(STORE_ROPE[kind, i, j])

from contextlib import ExitStack

import concourse.mybir as mybir
from concourse.masks import make_identity

F32 = mybir.dt.float32
BF16 = mybir.dt.bfloat16
U32 = mybir.dt.uint32
U8 = mybir.dt.uint8
I32 = mybir.dt.int32
FP8 = mybir.dt.float8_e4m3fn
FP8X4 = mybir.dt.float8_e4m3fn_x4
FP4X4 = mybir.dt.float4_e2m1fn_x4
ACT = mybir.ActivationFunctionType
ALU = mybir.AluOpType

P = 128
T, C, LORA, ROPE, KVW = 512, 2048, 512, 128, 4096
NT = T // P
G = C // 512
CKV = LORA + ROPE
BANK = 512
FLOPS = 2 * T * C * CKV + 2 * T * LORA * KVW
EPS = 1e-6
LAST_T0 = 1
WARM = (3, 2)
STORE_ROPE = {("o", 1, 1): 1, ("o", 3, 0): 3}
ORDER = [
    ("w", 0, 3, 1),
    ("w", 0, 0, 1),
    ("w", 0, 2, 0),
    ("T", 0, 3, 2),
    ("w", 0, 1, 0),
    ("T", 0, 0, 2),
    ("p", 0, 3, 1),
    ("p", 0, 0, 1),
    ("q", 0, 3, 1),
    ("T", 0, 2, 2),
    ("p", 0, 2, 1),
    ("T", 0, 1, 2),
    ("gain", 0, 0, 0),
    ("w", 1, 1, 1),
    ("p", 0, 1, 1),
    ("w", 1, 0, 0),
    ("m", 0, 3, 2),
    ("w", 1, 3, 1),
    ("w", 1, 2, 0),
    ("T", 1, 0, 2),
    ("T", 1, 1, 2),
    ("q", 0, 2, 1),
    ("q", 0, 0, 1),
    ("T", 1, 2, 2),
    ("T", 1, 3, 2),
    ("m", 0, 2, 2),
    ("m", 0, 0, 2),
    ("m", 0, 1, 2),
    ("p", 1, 0, 1),
    ("w", 2, 3, 0),
    ("p", 1, 1, 1),
    ("p", 1, 3, 1),
    ("p", 1, 2, 1),
    ("q", 1, 0, 1),
    ("w", 2, 1, 0),
    ("w", 2, 0, 0),
    ("r", 0, 0, 2),
    ("T", 2, 0, 2),
    ("T", 2, 1, 2),
    ("w", 2, 2, 0),
    ("q", 1, 2, 1),
    ("sq", 0, 0, 0),
    ("sr", 0, 0, 0),
    ("n", 0, 0, 1),
    ("w", 3, 3, 0),
    ("T", 2, 2, 2),
    ("T", 2, 3, 2),
    ("w", 3, 1, 0),
    ("m", 1, 0, 2),
    ("m", 1, 1, 2),
    ("t", 0, 0, 2),
    ("w", 3, 0, 0),
    ("p", 2, 1, 1),
    ("p", 2, 0, 1),
    ("p", 2, 3, 1),
    ("e", 0, 0, 0),
    ("z", 0, 0, 1),
    ("m", 1, 2, 2),
    ("m", 1, 3, 2),
    ("T", 3, 0, 2),
    ("T", 3, 1, 2),
    ("w", 3, 2, 0),
    ("q", 2, 0, 1),
    ("kc", 0, 0, 1),
    ("k", 0, 0, 2),
    ("p", 2, 2, 1),
    ("k", 0, 1, 2),
    ("k", 0, 2, 2),
    ("sq", 1, 0, 0),
    ("m", 2, 0, 2),
    ("m", 2, 1, 2),
    ("sr", 1, 0, 0),
    ("c", 0, 0, 0),
    ("o", 0, 0, 3),
    ("k", 0, 3, 2),
    ("c", 0, 1, 0),
    ("o", 0, 4, 3),
    ("n", 1, 0, 1),
    ("k", 0, 4, 2),
    ("T", 3, 2, 2),
    ("T", 3, 3, 2),
    ("c", 0, 2, 0),
    ("t", 1, 0, 2),
    ("k", 0, 5, 2),
    ("q", 2, 2, 1),
    ("c", 0, 3, 0),
    ("o", 0, 1, 3),
    ("k", 0, 6, 2),
    ("p", 3, 1, 1),
    ("p", 3, 0, 1),
    ("c", 0, 4, 0),
    ("p", 3, 3, 1),
    ("k", 0, 7, 2),
    ("e", 1, 0, 0),
    ("c", 0, 5, 0),
    ("o", 0, 2, 3),
    ("q", 3, 0, 1),
    ("m", 2, 2, 2),
    ("m", 2, 3, 2),
    ("r", 1, 0, 2),
    ("z", 1, 0, 1),
    ("c", 0, 6, 1),
    ("k", 1, 0, 2),
    ("p", 3, 2, 1),
    ("c", 0, 7, 0),
    ("o", 0, 3, 3),
    ("k", 1, 1, 2),
    ("kc", 1, 0, 1),
    ("k", 1, 2, 2),
    ("sq", 2, 0, 0),
    ("m", 3, 0, 2),
    ("m", 3, 1, 2),
    ("c", 1, 0, 0),
    ("sr", 2, 0, 0),
    ("k", 1, 3, 2),
    ("c", 1, 1, 1),
    ("o", 1, 0, 3),
    ("n", 2, 0, 1),
    ("k", 1, 4, 2),
    ("c", 1, 2, 0),
    ("k", 1, 5, 2),
    ("t", 2, 0, 2),
    ("q", 3, 2, 1),
    ("c", 1, 3, 0),
    ("o", 1, 1, 3),
    ("k", 1, 6, 2),
    ("c", 1, 4, 1),
    ("k", 1, 7, 2),
    ("c", 1, 5, 0),
    ("o", 1, 2, 3),
    ("e", 2, 0, 0),
    ("m", 3, 2, 2),
    ("m", 3, 3, 2),
    ("r", 2, 0, 2),
    ("z", 2, 0, 1),
    ("c", 1, 6, 0),
    ("k", 2, 0, 2),
    ("c", 1, 7, 1),
    ("o", 1, 3, 3),
    ("k", 2, 1, 2),
    ("kc", 2, 0, 1),
    ("k", 2, 2, 2),
    ("sq", 3, 0, 0),
    ("c", 2, 0, 0),
    ("sr", 3, 0, 0),
    ("k", 2, 3, 2),
    ("c", 2, 1, 1),
    ("o", 2, 0, 3),
    ("n", 3, 0, 1),
    ("k", 2, 4, 2),
    ("c", 2, 2, 0),
    ("k", 2, 5, 2),
    ("t", 3, 0, 2),
    ("c", 2, 3, 0),
    ("o", 2, 1, 3),
    ("k", 2, 6, 2),
    ("c", 2, 4, 1),
    ("k", 2, 7, 2),
    ("c", 2, 5, 0),
    ("o", 2, 2, 3),
    ("e", 3, 0, 0),
    ("r", 3, 0, 2),
    ("z", 3, 0, 1),
    ("c", 2, 6, 0),
    ("k", 3, 0, 2),
    ("c", 2, 7, 1),
    ("o", 2, 3, 3),
    ("k", 3, 1, 2),
    ("kc", 3, 0, 1),
    ("k", 3, 2, 2),
    ("c", 3, 0, 0),
    ("k", 3, 3, 2),
    ("c", 3, 1, 1),
    ("o", 3, 0, 3),
    ("k", 3, 4, 2),
    ("c", 3, 2, 0),
    ("k", 3, 5, 2),
    ("c", 3, 3, 0),
    ("o", 3, 1, 3),
    ("k", 3, 6, 2),
    ("c", 3, 4, 1),
    ("k", 3, 7, 2),
    ("c", 3, 5, 0),
    ("o", 3, 2, 3),
    ("c", 3, 6, 0),
    ("o", 3, 3, 3),
    ("c", 3, 7, 1),
    ("o", 3, 4, 3),
]


def tile_multiheadlatentattention_pa_w4_kernel(
    tc, x_bytes, x_scale, freq_cis, Wckv_words, Wckv_scales, kv_norm_w, Wdkv_words, Wdkv_scales, out_0, out_1
):
    nc = tc.nc
    with ExitStack() as ctx:
        keep = ctx.enter_context(tc.tile_pool(name="keep", bufs=1))
        work = ctx.enter_context(tc.tile_pool(name="work", bufs=4))
        outs = ctx.enter_context(tc.tile_pool(name="outs", bufs=16))
        ps_x = ctx.enter_context(tc.psum_pool(name="ps_x", bufs=2))
        ps_l = ctx.enter_context(tc.psum_pool(name="ps_l", bufs=2))
        ps_k = ctx.enter_context(tc.psum_pool(name="ps_k", bufs=4))

        xb = keep.tile([P, NT, C], U8, name="xb", align_bytes=64)
        sc = keep.tile([P, G, 8], F32, name="sc", align_bytes=64)
        wa = keep.tile([P, G, 2 * CKV], U8, name="wa", align_bytes=64)
        wa_s = keep.tile([P, G, CKV], U8, name="wa_s", align_bytes=64)
        wb = keep.tile([P, 2 * KVW], U8, name="wb", align_bytes=64)
        wb_s = keep.tile([P, KVW], U8, name="wb_s", align_bytes=64)
        fr = keep.tile([P, NT, ROPE // 2, 2], BF16, name="fr")
        ident = keep.tile([P, P], F32, name="ident")
        row = keep.tile([P, LORA], BF16, name="row")
        ones = keep.tile([P, BANK], BF16, name="ones")
        gain = keep.tile([P, LORA], BF16, name="gain")
        ss = keep.tile([P, NT], F32, name="ss")
        rs = keep.tile([P, NT], F32, name="rs")
        ra = keep.tile([P, NT, ROPE], F32, name="ra")
        rb = keep.tile([P, NT, ROPE], F32, name="rb")
        ro = keep.tile([P, NT, ROPE], F32, name="ro")
        dummy = keep.tile([P, 1], F32, name="dummy")

        wa_s32 = wa_s[:].rearrange("p g n -> p (g n)").bitcast(I32)
        make_identity(nc, ident[:])
        nc.vector.memset(row[:], 0.0)
        nc.scalar.dma_start(out=row[0:1, :], in_=kv_norm_w.rearrange("(o n) -> o n", o=1))
        nc.vector.memset(wa_s32, 0)
        nc.vector.memset(ones[:], 1.0)
        nc.vector.memset(dummy[:], 1.0)
        nc.vector.memset(wb_s[:].bitcast(I32), 0)
        nc.scalar.activation(out=dummy[:], in_=dummy[:], func=ACT.Abs_reciprocal_sqrt)

        def load_x(i, c0, c1):
            nc.sync.dma_start(out=xb[:, i, c0:c1], in_=x_bytes[0, i * P : (i + 1) * P, c0:c1])

        load_x(0, 0, 2048)
        nc.sync.dma_start(out=sc[:, :, 0:4], in_=x_scale.rearrange("a b (g p t) -> p (a b g) t", p=P, t=4))
        wa_s3 = wa_s32.rearrange("p (g n) -> p g n", g=G)
        src = Wckv_scales.bitcast(I32).rearrange("g (q r) n -> r q g n", r=4)
        for r in range(4):
            nc.sync.dma_start(out=wa_s3[r:P:32], in_=src[r])
        nc.sync.dma_start(out=wa[:], in_=Wckv_words.rearrange("g p c -> p g c"))
        load_x(1, 0, 2048)
        nc.gpsimd.dma_start(out=fr[:], in_=freq_cis.rearrange("(i p) h c -> p i h c", p=P))
        load_x(2, 0, 2048)
        src = Wdkv_scales.bitcast(I32).rearrange("g (q r) n -> r (g q) n", r=4)
        for r in range(4):
            nc.sync.dma_start(out=wb_s[:].bitcast(I32)[r:P:32], in_=src[r])
        for h in range(2):
            nc.sync.dma_start(out=wb[:, h * KVW : (h + 1) * KVW], in_=Wdkv_words[0, :, h * KVW : (h + 1) * KVW])
        load_x(3, 0, 2048)

        def warm(n):
            hot = ps_k.tile([P, BANK], F32, name="kvb")
            for _ in range(n):
                nc.tensor.matmul(hot[:], lhsT=ones[:, 0:P], rhs=ones[:], start=True, stop=True)

        xw, xg, xt, codes, scales, lat, nb, nt, ng, ncodes, nscales, kr, kv, ob = ({} for _ in range(14))

        def gain_matmul():
            bank = ps_k.tile([P, BANK], F32, name="kvb")
            nc.tensor.matmul(bank[:], lhsT=ones[:, 0:P], rhs=row[:], start=True, stop=True)
            return bank

        def do_gain(bank):
            nc.scalar.copy(out=gain[:], in_=bank[:])

        def do_w(i, g, eng):
            if i not in xw:
                xw[i] = work.tile([P, C], BF16, name="xwt")
            c = slice(512 * g, 512 * (g + 1))
            src = xb[:, i, c].bitcast(FP8)
            if eng == 0:
                nc.scalar.copy(out=xw[i][:, c], in_=src)
            else:
                nc.vector.tensor_copy(out=xw[i][:, c], in_=src)

        def do_T(i, g):
            if i == 0:
                if g < 2:
                    bank = ps_x.tile([P, BANK], F32, name="xtb")
                else:
                    bank = ps_k.tile([P, BANK], F32, name="kvb")
                xt[i, g] = bank[:, 0:256]
            elif (i, g) not in xt:
                bank = ps_x.tile([P, BANK], F32, name="xtb")
                for k in range(2):
                    xt[i, (g & 2) + k] = bank[:, 256 * k : 256 * (k + 1)]
            words = xw[i][:].bitcast(F32)
            for u in range(2):
                nc.tensor.transpose(xt[i, g][:, P * u : P * (u + 1)], words[:, 256 * g + u : 256 * (g + 1) : 2], ident[:])

        def do_p(i, g, eng):
            if i not in xg:
                xg[i] = work.tile([P, G, P, 4], BF16, name="xgt", align_bytes=64)
            if eng == 0:
                for u in range(2):
                    for e in range(2):
                        nc.scalar.activation(
                            out=xg[i][:, g, :, 2 * u + e : 2 * u + e + 1],
                            in_=xt[i, g].bitcast(BF16).rearrange("p (u r e) -> p u r e", u=2, e=2)[:, u, :, e : e + 1],
                            func=ACT.Copy,
                            scale=sc[:, g, 2 * u + e : 2 * u + e + 1],
                        )
                return
            nc.vector.tensor_tensor(
                out=xg[i][:, g].rearrange("p r (u e) -> p r u e", e=2),
                in0=xt[i, g].bitcast(BF16).rearrange("p (u r e) -> p r u e", u=2, e=2),
                in1=sc[:, g : g + 1, 0:4].rearrange("p o (u e) -> p o u e", e=2).to_broadcast([P, P, 2, 2]),
                op=ALU.mult,
            )

        def do_q(i, g):
            if i not in codes:
                codes[i] = work.tile([P, G, P], U32, name="codest", align_bytes=64)
                scales[i] = work.tile([P, G, P], U8, name="scalest", align_bytes=64)
            n = 1 if i == 0 and g >= 2 else 2
            gs = slice(g, g + n)
            nc.vector.quantize_mx(
                out=codes[i][:, gs].rearrange("p g r -> p (g r)").bitcast(FP8X4),
                scales=scales[i][:, gs].rearrange("p g r -> p (g r)"),
                in_=xg[i][:, gs].rearrange("p g r t -> p (g r t)"),
            )

        order_m = {}

        def mm1(i, g, dst, c0, n, start, stop):
            nc.tensor.matmul_mx(
                out=dst,
                lhsT=codes[i][:, g].bitcast(FP8X4),
                lhsT_scale=scales[i][:, g],
                rhs=wa[:, g, 2 * c0 : 2 * (c0 + n)].bitcast(FP4X4),
                rhs_scale=wa_s[:, g, c0 : c0 + n],
                start=start,
                stop=stop,
            )

        def do_m(i, g):
            if i not in lat:
                lat[i] = ps_l.tile([P, LORA], F32, name="latt")
                order_m[i] = 0
            mm1(i, g, lat[i][:], 0, LORA, order_m[i] == 0, order_m[i] == G - 1)
            order_m[i] += 1

        def do_r(i):
            kr[i] = ps_k.tile([P, BANK], F32, name="kvb")
            for g in range(G):
                mm1(i, g, kr[i][:, 0:ROPE], LORA, ROPE, g == 0, g == G - 1)

        def do_kc(i):
            shape = [P, ROPE // 2, 2]
            pairs = kr[i][:, 0:ROPE].rearrange("p (h e) -> p h e", e=2)
            for dst, c in ((ra, 0), (rb, 1)):
                nc.vector.tensor_tensor(
                    out=dst[:, i].rearrange("p (h e) -> p h e", e=2),
                    in0=pairs,
                    in1=fr[:, i, :, c : c + 1].to_broadcast(shape),
                    op=ALU.mult,
                )
            if i % 2:
                a2, b2, o2 = (v[:, i - 1 : i + 1].rearrange("p i (h e) -> p (i h) e", e=2) for v in (ra, rb, ro))
                nc.vector.tensor_tensor(out=o2[:, :, 0:1], in0=a2[:, :, 0:1], in1=b2[:, :, 1:2], op=ALU.subtract)
                nc.vector.tensor_tensor(out=o2[:, :, 1:2], in0=a2[:, :, 1:2], in1=b2[:, :, 0:1], op=ALU.add)

        def do_rope_store(i):
            nc.sync.dma_start(
                out=out_1[0, (i - 1) * P : (i + 1) * P, :].rearrange("(i p) c -> p i c", p=P), in_=ro[:, i - 1 : i + 1]
            )

        def do_sq(i):
            junk = work.tile([P, LORA], F32, name="junk")
            nc.scalar.activation(out=junk[:], in_=lat[i][:], func=ACT.Square, accum_out=ss[:, i : i + 1])

        def do_sr(i):
            nc.scalar.activation(
                out=rs[:, i : i + 1], in_=ss[:, i : i + 1], func=ACT.Abs_reciprocal_sqrt, scale=1.0 / LORA, bias=EPS
            )

        def do_n(i):
            nb[i] = work.tile([P, LORA], BF16, name="nbt")
            nc.vector.scalar_tensor_tensor(
                out=nb[i][:], in0=lat[i][:], scalar=rs[:, i : i + 1], in1=gain[:], op0=ALU.mult, op1=ALU.mult
            )

        def do_t(i):
            nt[i] = ps_k.tile([P, BANK], F32, name="kvb")
            words = nb[i][:].bitcast(F32)
            for u in range(2):
                nc.tensor.transpose(nt[i][:, P * u : P * (u + 1)], words[:, u:256:2], ident[:])

        def do_e(i):
            ng[i] = work.tile([P, 4 * P], BF16, name="ngt", align_bytes=64)
            nc.scalar.copy(
                out=ng[i][:].bitcast(F32).rearrange("p (r u) -> p r u", u=2),
                in_=nt[i][:, 0:256].rearrange("p (u r) -> p r u", u=2),
            )

        def do_z(i):
            ncodes[i] = work.tile([P, P], U32, name="ncodest", align_bytes=64)
            nscales[i] = work.tile([P, P], U8, name="nscalest", align_bytes=64)
            nc.vector.quantize_mx(out=ncodes[i][:].bitcast(FP8X4), scales=nscales[i][:], in_=ng[i][:])

        def do_k(i, j):
            kv[i, j] = ps_k.tile([P, BANK], F32, name="kvb")
            nc.tensor.matmul_mx(
                out=kv[i, j][:],
                lhsT=ncodes[i][:].bitcast(FP8X4),
                lhsT_scale=nscales[i][:],
                rhs=wb[:, 2 * BANK * j : 2 * BANK * (j + 1)].bitcast(FP4X4),
                rhs_scale=wb_s[:, BANK * j : BANK * (j + 1)],
                start=True,
                stop=True,
            )

        def do_c(i, j, eng):
            h, k = divmod(j, 2)
            if (i, h) not in ob:
                ob[i, h] = outs.tile([P, 2, BANK], F32, name="obt")
            if eng == 1:
                nc.vector.tensor_copy(out=ob[i, h][:, k], in_=kv[i, j][:])
            else:
                nc.scalar.copy(out=ob[i, h][:, k], in_=kv[i, j][:])

        def do_o(i, h):
            rows = slice(i * P, (i + 1) * P)
            b, lo, hi = h, 0, 2
            if (i, h) == (0, 0):
                hi = 1
            elif (i, h) == (0, 4):
                b, lo = 0, 1
            elif (i, h) == (3, 3):
                hi = 1
            elif (i, h) == (3, 4):
                b, lo = 3, 1
            nc.sync.dma_start(
                out=out_0[0, rows, BANK * (2 * b + lo) : BANK * (2 * b + hi)],
                in_=ob[i, b][:, lo:hi].rearrange("p k n -> p (k n)"),
            )

        table = {
            "w": do_w, "T": do_T, "p": do_p, "q": do_q, "m": do_m, "r": do_r, "kc": do_kc, "sq": do_sq, "sr": do_sr,
            "n": do_n, "t": do_t, "e": do_e, "z": do_z, "k": do_k, "c": do_c, "o": do_o,
        }
        with tc.manual_schedule():
            warm(WARM[0])
            for kind, i, j, eng in ORDER:
                if kind == "gain":
                    do_gain(gain_bank)
                elif kind in ("w", "c", "p"):
                    table[kind](i, j, eng)
                elif kind in ("T", "q", "m", "k", "o"):
                    table[kind](i, j)
                else:
                    table[kind](i)
                if kind == "T" and len(xt) == 1:
                    gain_bank = gain_matmul()
                if (kind, i, j) == ("T", 0, LAST_T0):
                    warm(WARM[1])
                if (kind, i, j) in STORE_ROPE:
                    do_rope_store(STORE_ROPE[kind, i, j])
